import numpy as np
import ml_dtypes


def mxq(x, axis, fmt="e4m3"):
    dtype, down = {"e4m3": (ml_dtypes.float8_e4m3fn, 7), "e5m2": (ml_dtypes.float8_e5m2, 14)}[fmt]
    v = np.moveaxis(np.asarray(x, np.float32).astype(ml_dtypes.bfloat16).astype(np.float64), axis, -1)
    blocks = v.reshape(v.shape[:-1] + (-1, 32))
    amax = np.abs(blocks).max(-1, keepdims=True)
    byte = np.maximum(np.where(amax > 0, np.frexp(amax)[1] - 1 + 127, 0) - down, 1)
    scale = np.exp2(byte - 127.0)
    codes = (blocks / scale).astype(np.float32).astype(dtype).astype(np.float64)
    return np.moveaxis((codes * scale).reshape(v.shape), -1, axis)


WIDE = False


def mx_kscale(k):
    if not WIDE:
        return np.ones(k)
    levels = np.array([10, -10, 5, -5, 0])
    a = np.random.permutation(np.resize(levels, k // 512 * 4)).reshape(k // 512, 4)
    idx = np.arange(k)
    return np.exp2(a[idx // 512, idx % 128 // 32])


BF16 = ml_dtypes.bfloat16


def bf(x):
    return np.asarray(x, np.float32).astype(BF16)


def f64(x):
    return np.asarray(x).astype(np.float64)


N, Ci, H, W, Co = 4, 1024, 32, 32, 256
TAPS = [(1, 1), (0, 1), (1, 0), (1, 2), (2, 1)]
K = len(TAPS)
PAD = 1


def setup_inputs():
    s = mx_kscale(Ci)
    return {"x": bf(np.random.standard_normal((N, Ci, H, W)) * s[None, :, None, None]),
            "weight": bf(np.random.standard_normal((Co, Ci, K)) / np.sqrt(Ci * K) / s[None, :, None])}


def reference(x, weight):
    xq = mxq(f64(x).reshape(N, Ci, H * W), 1, "e4m3")
    wq = mxq(f64(weight), 1, "e4m3")
    outs = []
    for k, (dy, dx) in enumerate(TAPS):
        y = (wq[:, :, k] @ xq).reshape(N, Co, H, W)
        yp = np.pad(y, ((0, 0), (0, 0), (PAD, PAD), (PAD, PAD)))
        outs.append(yp[:, :, dy:dy + H, dx:dx + W])
    return np.stack(outs, axis=0).sum(axis=0)

@@ -1,0 +1,216 @@
+from contextlib import ExitStack
+
+import concourse.mybir as mybir
+from concourse.masks import make_identity
+
+BF16 = mybir.dt.bfloat16
+F32 = mybir.dt.float32
+I32 = mybir.dt.int32
+U32 = mybir.dt.uint32
+U8 = mybir.dt.uint8
+FP8X4 = mybir.dt.float8_e4m3fn_x4
+ADD = mybir.AluOpType.add
+
+IMAGES, C_IN, HEIGHT, WIDTH = 4, 1024, 32, 32
+C_OUT, TAPS = 256, 5
+P = 128
+PACK = 4
+K_PASS = P * PACK
+PASSES = C_IN // K_PASS
+O_TILES = C_OUT // P
+HALVES = 2
+HALF_ROWS = HEIGHT // HALVES
+HALF_PIX = HALF_ROWS * WIDTH
+PAD_PIX = (HEIGHT + 2) * WIDTH
+OPERANDS = PASSES * TAPS
+
+CENTRE, UP, LEFT, RIGHT, DOWN = 0, 1, 2, 3, 4
+ROW_OFFSET = {CENTRE: 0, UP: -1, LEFT: 0, RIGHT: 0, DOWN: 1}
+
+VECTOR_PIX = 192
+
+FLOPS = 2 * IMAGES * HEIGHT * WIDTH * C_IN * C_OUT * TAPS
+
+
+def tile_spatialconv_pa_t_kernel(tc, x, weight, out):
+    nc = tc.nc
+    with ExitStack() as ctx:
+        keep = ctx.enter_context(tc.tile_pool(name="keep", bufs=1))
+        stage = ctx.enter_context(tc.tile_pool(name="stage", bufs=4))
+        acc_pool = ctx.enter_context(tc.psum_pool(name="acc", bufs=2))
+        flip_pool = ctx.enter_context(tc.psum_pool(name="flip", bufs=2))
+
+        w_raw = {}
+        x_raw = {}
+
+        def load_weights(m):
+            for g in range(PASSES):
+                w_raw[m, g] = keep.tile([P, K_PASS * TAPS], BF16, name="w_raw_%d_%d" % (m, g))
+                nc.sync.dma_start(
+                    out=w_raw[m, g][:],
+                    in_=weight[m * P : (m + 1) * P, g * K_PASS : (g + 1) * K_PASS, :].rearrange(
+                        "o c k -> o (c k)"
+                    ),
+                )
+
+        def load_image(n):
+            for half in range(HALVES):
+                for g in range(PASSES):
+                    x_raw[n, half, g] = keep.tile(
+                        [P, PACK, HALF_PIX], BF16, name="x_raw_%d_%d_%d" % (n, half, g)
+                    )
+                    nc.sync.dma_start(
+                        out=x_raw[n, half, g][:],
+                        in_=x[
+                            n,
+                            g * K_PASS : (g + 1) * K_PASS,
+                            half * HALF_ROWS : (half + 1) * HALF_ROWS,
+                            :,
+                        ].rearrange("(p j) h w -> p j (h w)", j=PACK),
+                    )
+
+        load_weights(0)
+        load_image(0)
+        load_weights(1)
+        for n in range(1, IMAGES):
+            load_image(n)
+
+        ident = keep.tile([P, P], F32, name="ident")
+        make_identity(nc, ident[:])
+
+        x_codes = {}
+        x_scales = {}
+        x_scales_pad = {}
+        for n in range(IMAGES):
+            x_codes[n] = keep.tile([P, PASSES, PAD_PIX], U32, name="x_codes_%d" % n, align_bytes=64)
+            x_scales[n] = keep.tile(
+                [P, PASSES, HEIGHT * WIDTH], U8, name="x_scales_%d" % n, align_bytes=64
+            )
+            x_scales_pad[n] = keep.tile(
+                [P, PASSES, PAD_PIX], U8, name="x_scales_pad_%d" % n, align_bytes=64
+            )
+            nc.vector.memset(x_scales[n][:].bitcast(I32), 0)
+            nc.vector.memset(x_scales_pad[n][:].bitcast(I32), 0)
+            nc.vector.memset(x_codes[n][:, :, 0:WIDTH].bitcast(I32), 0)
+            nc.vector.memset(x_codes[n][:, :, PAD_PIX - WIDTH : PAD_PIX].bitcast(I32), 0)
+
+        w_codes = {}
+        w_scales = {}
+
+        def prepare_weights(m):
+            sorted_w = keep.tile([P, OPERANDS, 2, 2 * P], BF16, name="sorted_w_%d" % m)
+            for g in range(PASSES):
+                by_tap = w_raw[m, g][:].rearrange("o (p u e k) -> o k u p e", u=2, e=2, k=TAPS)
+                for u, engine_copy in ((0, nc.vector.tensor_copy), (1, nc.scalar.copy)):
+                    engine_copy(
+                        out=sorted_w[:, g * TAPS : (g + 1) * TAPS, u, :].rearrange(
+                            "o k (p e) -> o k p e", e=2
+                        ),
+                        in_=by_tap[:, :, u],
+                    )
+            sorted_words = sorted_w[:].bitcast(F32)
+            grouped_w = keep.tile([P, OPERANDS, PACK * P], BF16, name="grouped_w_%d" % m, align_bytes=64)
+            grouped_words = grouped_w[:].bitcast(F32)
+            w_codes[m] = keep.tile([P, OPERANDS, P], U32, name="w_codes_%d" % m, align_bytes=64)
+            w_scales[m] = keep.tile([P, OPERANDS, P], U8, name="w_scales_%d" % m, align_bytes=64)
+            for first in range(0, OPERANDS, 2):
+                pair = slice(first, first + 2)
+                flipped = flip_pool.tile([P, 2, 2, P], F32, name="flipped")
+                for a in range(2):
+                    for u in range(2):
+                        nc.tensor.transpose(
+                            out=flipped[:, a, u, :], in_=sorted_words[:, first + a, u, :], identity=ident[:]
+                        )
+                engine_copy = nc.scalar.copy if first % 4 == 0 else nc.vector.tensor_copy
+                engine_copy(
+                    out=grouped_words[:, pair, :].rearrange("p a (o u) -> p a o u", u=2),
+                    in_=flipped[:].rearrange("p a u o -> p a o u"),
+                )
+                nc.vector.quantize_mx(
+                    out=w_codes[m][:, pair, :].rearrange("p a o -> p (a o)").bitcast(FP8X4),
+                    scales=w_scales[m][:, pair, :].rearrange("p a o -> p (a o)"),
+                    in_=grouped_w[:, pair, :].rearrange("p a f -> p (a f)"),
+                )
+
+        def prepare_piece(n, half, g):
+            raw = x_raw[n, half, g]
+            grouped = stage.tile([P, HALF_PIX, PACK], BF16, name="grouped", align_bytes=64)
+            for cols, engine_copy in (
+                (slice(0, VECTOR_PIX), nc.vector.tensor_copy),
+                (slice(VECTOR_PIX, HALF_PIX), nc.scalar.copy),
+            ):
+                engine_copy(
+                    out=grouped[:, cols, :].rearrange("p (c i) j -> p c j i", i=4),
+                    in_=raw[:, :, cols].rearrange("p j (c i) -> p c j i", i=4),
+                )
+            first = half * HALF_PIX
+            nc.vector.quantize_mx(
+                out=x_codes[n][:, g, WIDTH + first : WIDTH + first + HALF_PIX].bitcast(FP8X4),
+                scales=x_scales[n][:, g, first : first + HALF_PIX],
+                in_=grouped[:].rearrange("p w j -> p (w j)"),
+            )
+            nc.vector.tensor_copy(
+                out=x_scales_pad[n][:, g, WIDTH + first : WIDTH + first + HALF_PIX].bitcast(I32),
+                in_=x_scales[n][:, g, first : first + HALF_PIX].bitcast(I32),
+            )
+
+        def tap_passes(acc, n, m, half, taps):
+            last = len(taps) * PASSES - 1
+            count = 0
+            for tap in taps:
+                first_row = half * HALF_ROWS + ROW_OFFSET[tap]
+                first = (first_row + 1) * WIDTH
+                for g in range(PASSES):
+                    if first_row % 2 == 0:
+                        plane = x_scales[n][:, g, first - WIDTH : first - WIDTH + HALF_PIX]
+                    else:
+                        plane = x_scales_pad[n][:, g, first : first + HALF_PIX]
+                    nc.tensor.matmul_mx(
+                        out=acc[:].rearrange("o h w -> o (h w)"),
+                        lhsT=w_codes[m][:, g * TAPS + tap, :].bitcast(FP8X4),
+                        lhsT_scale=w_scales[m][:, g * TAPS + tap, :],
+                        rhs=x_codes[n][:, g, first : first + HALF_PIX].bitcast(FP8X4),
+                        rhs_scale=plane,
+                        start=(count == 0),
+                        stop=(count == last),
+                    )
+                    count += 1
+
+        def convolve(n, m, half):
+            acc_mid = acc_pool.tile([P, HALF_ROWS, WIDTH], F32, name="acc_mid")
+            tap_passes(acc_mid, n, m, half, (CENTRE, UP, DOWN))
+            acc_left = acc_pool.tile([P, HALF_ROWS, WIDTH], F32, name="acc_left")
+            tap_passes(acc_left, n, m, half, (LEFT,))
+            acc_right = acc_pool.tile([P, HALF_ROWS, WIDTH], F32, name="acc_right")
+            tap_passes(acc_right, n, m, half, (RIGHT,))
+            result = stage.tile([P, HALF_ROWS, WIDTH], F32, name="result")
+            nc.scalar.copy(out=result[:], in_=acc_mid[:])
+            nc.vector.tensor_tensor(
+                out=result[:, :, 1:WIDTH],
+                in0=acc_left[:, :, 0 : WIDTH - 1],
+                in1=result[:, :, 1:WIDTH],
+                op=ADD,
+            )
+            nc.vector.tensor_tensor(
+                out=result[:, :, 0 : WIDTH - 1],
+                in0=acc_right[:, :, 1:WIDTH],
+                in1=result[:, :, 0 : WIDTH - 1],
+                op=ADD,
+            )
+            nc.sync.dma_start(
+                out=out[n, m * P : (m + 1) * P, half * HALF_ROWS : (half + 1) * HALF_ROWS, :],
+                in_=result[:],
+            )
+
+        pieces = [(half, g) for half in range(HALVES) for g in range(PASSES)]
+        rounds = [(m, half) for m in range(O_TILES) for half in range(HALVES)]
+        prepare_weights(0)
+        for half, g in pieces:
+            prepare_piece(0, half, g)
+        for n in range(IMAGES):
+            for (m, half), (next_half, next_g) in zip(rounds, pieces):
+                convolve(n, m, half)
+                if n == 0 and half == 0 and m + 1 < O_TILES:
+                    prepare_weights(m + 1)
+                if n + 1 < IMAGES:
+                    prepare_piece(n + 1, next_half, next_g)

@@ -21,11 +21,18 @@ O_TILES = C_OUT // P
 HALVES = 2
 HALF_ROWS = HEIGHT // HALVES
 HALF_PIX = HALF_ROWS * WIDTH
+IMAGE_PIX = HEIGHT * WIDTH
 PAD_PIX = (HEIGHT + 2) * WIDTH
 OPERANDS = PASSES * TAPS
+PSUM_BANKS = 8
 
 CENTRE, UP, LEFT, RIGHT, DOWN = 0, 1, 2, 3, 4
 ROW_OFFSET = {CENTRE: 0, UP: -1, LEFT: 0, RIGHT: 0, DOWN: 1}
+MID_TAPS, LEFT_TAPS, RIGHT_TAPS = (CENTRE, UP, DOWN), (LEFT,), (RIGHT,)
+
+STEPS = IMAGES * O_TILES * PASSES
+PIECES = IMAGES * PASSES * HALVES
+ROUNDS = IMAGES * O_TILES * HALVES
 
 VECTOR_PIX = 192
 
@@ -37,13 +44,11 @@ def tile_spatialconv_pa_t_kernel(tc, x, weight, out):
     with ExitStack() as ctx:
         keep = ctx.enter_context(tc.tile_pool(name="keep", bufs=1))
         stage = ctx.enter_context(tc.tile_pool(name="stage", bufs=4))
-        acc_pool = ctx.enter_context(tc.psum_pool(name="acc", bufs=2))
-        flip_pool = ctx.enter_context(tc.psum_pool(name="flip", bufs=2))
+        psum = ctx.enter_context(tc.psum_pool(name="psum", bufs=PSUM_BANKS))
+        ctx.enter_context(tc.manual_schedule())
 
         w_raw = {}
-        x_raw = {}
-
-        def load_weights(m):
+        for m in range(O_TILES):
             for g in range(PASSES):
                 w_raw[m, g] = keep.tile([P, K_PASS * TAPS], BF16, name="w_raw_%d_%d" % (m, g))
                 nc.sync.dma_start(
@@ -52,28 +57,16 @@ def tile_spatialconv_pa_t_kernel(tc, x, weight, out):
                         "o c k -> o (c k)"
                     ),
                 )
-
-        def load_image(n):
-            for half in range(HALVES):
-                for g in range(PASSES):
-                    x_raw[n, half, g] = keep.tile(
-                        [P, PACK, HALF_PIX], BF16, name="x_raw_%d_%d_%d" % (n, half, g)
-                    )
-                    nc.sync.dma_start(
-                        out=x_raw[n, half, g][:],
-                        in_=x[
-                            n,
-                            g * K_PASS : (g + 1) * K_PASS,
-                            half * HALF_ROWS : (half + 1) * HALF_ROWS,
-                            :,
-                        ].rearrange("(p j) h w -> p j (h w)", j=PACK),
-                    )
-
-        load_weights(0)
-        load_image(0)
-        load_weights(1)
-        for n in range(1, IMAGES):
-            load_image(n)
+        x_raw = {}
+        for j in range(PIECES):
+            n, g, half = j // 4, (j // 2) % 2, j % 2
+            x_raw[j] = keep.tile([P, PACK, HALF_PIX], BF16, name="x_raw_%d" % j)
+            nc.sync.dma_start(
+                out=x_raw[j][:],
+                in_=x[
+                    n, g * K_PASS : (g + 1) * K_PASS, half * HALF_ROWS : (half + 1) * HALF_ROWS, :
+                ].rearrange("(p j) h w -> p j (h w)", j=PACK),
+            )
 
         ident = keep.tile([P, P], F32, name="ident")
         make_identity(nc, ident[:])
@@ -83,9 +76,7 @@ def tile_spatialconv_pa_t_kernel(tc, x, weight, out):
         x_scales_pad = {}
         for n in range(IMAGES):
             x_codes[n] = keep.tile([P, PASSES, PAD_PIX], U32, name="x_codes_%d" % n, align_bytes=64)
-            x_scales[n] = keep.tile(
-                [P, PASSES, HEIGHT * WIDTH], U8, name="x_scales_%d" % n, align_bytes=64
-            )
+            x_scales[n] = keep.tile([P, PASSES, IMAGE_PIX], U8, name="x_scales_%d" % n, align_bytes=64)
             x_scales_pad[n] = keep.tile(
                 [P, PASSES, PAD_PIX], U8, name="x_scales_pad_%d" % n, align_bytes=64
             )
@@ -94,123 +85,143 @@ def tile_spatialconv_pa_t_kernel(tc, x, weight, out):
             nc.vector.memset(x_codes[n][:, :, 0:WIDTH].bitcast(I32), 0)
             nc.vector.memset(x_codes[n][:, :, PAD_PIX - WIDTH : PAD_PIX].bitcast(I32), 0)
 
+        sorted_w = {}
+        grouped_w = {}
         w_codes = {}
         w_scales = {}
-
-        def prepare_weights(m):
-            sorted_w = keep.tile([P, OPERANDS, 2, 2 * P], BF16, name="sorted_w_%d" % m)
-            for g in range(PASSES):
-                by_tap = w_raw[m, g][:].rearrange("o (p u e k) -> o k u p e", u=2, e=2, k=TAPS)
-                for u, engine_copy in ((0, nc.vector.tensor_copy), (1, nc.scalar.copy)):
-                    engine_copy(
-                        out=sorted_w[:, g * TAPS : (g + 1) * TAPS, u, :].rearrange(
-                            "o k (p e) -> o k p e", e=2
-                        ),
-                        in_=by_tap[:, :, u],
-                    )
-            sorted_words = sorted_w[:].bitcast(F32)
-            grouped_w = keep.tile([P, OPERANDS, PACK * P], BF16, name="grouped_w_%d" % m, align_bytes=64)
-            grouped_words = grouped_w[:].bitcast(F32)
+        for m in range(O_TILES):
+            sorted_w[m] = keep.tile([P, OPERANDS, 2, 2 * P], BF16, name="sorted_w_%d" % m)
+            grouped_w[m] = keep.tile(
+                [P, OPERANDS, PACK * P], BF16, name="grouped_w_%d" % m, align_bytes=64
+            )
             w_codes[m] = keep.tile([P, OPERANDS, P], U32, name="w_codes_%d" % m, align_bytes=64)
             w_scales[m] = keep.tile([P, OPERANDS, P], U8, name="w_scales_%d" % m, align_bytes=64)
-            for first in range(0, OPERANDS, 2):
-                pair = slice(first, first + 2)
-                flipped = flip_pool.tile([P, 2, 2, P], F32, name="flipped")
-                for a in range(2):
-                    for u in range(2):
-                        nc.tensor.transpose(
-                            out=flipped[:, a, u, :], in_=sorted_words[:, first + a, u, :], identity=ident[:]
-                        )
-                engine_copy = nc.scalar.copy if first % 4 == 0 else nc.vector.tensor_copy
-                engine_copy(
-                    out=grouped_words[:, pair, :].rearrange("p a (o u) -> p a o u", u=2),
-                    in_=flipped[:].rearrange("p a u o -> p a o u"),
-                )
-                nc.vector.quantize_mx(
-                    out=w_codes[m][:, pair, :].rearrange("p a o -> p (a o)").bitcast(FP8X4),
-                    scales=w_scales[m][:, pair, :].rearrange("p a o -> p (a o)"),
-                    in_=grouped_w[:, pair, :].rearrange("p a f -> p (a f)"),
-                )
 
-        def prepare_piece(n, half, g):
-            raw = x_raw[n, half, g]
-            grouped = stage.tile([P, HALF_PIX, PACK], BF16, name="grouped", align_bytes=64)
+        def sort_weights(m, g):
+            nc.vector.tensor_copy(
+                out=sorted_w[m][:, g * TAPS : (g + 1) * TAPS, :, :].rearrange(
+                    "o k u (p e) -> o k u p e", e=2
+                ),
+                in_=w_raw[m, g][:].rearrange("o (p u e k) -> o k u p e", u=2, e=2, k=TAPS),
+            )
+
+        def flip_weights(m, first):
+            pair = slice(first, first + 2)
+            flipped = psum.tile([P, 2, 2, P], F32, name="flipped", tag="bank")
+            for a in range(2):
+                for u in range(2):
+                    nc.tensor.transpose(
+                        out=flipped[:, a, u, :],
+                        in_=sorted_w[m][:].bitcast(F32)[:, first + a, u, :],
+                        identity=ident[:],
+                    )
+            nc.scalar.copy(
+                out=grouped_w[m][:].bitcast(F32)[:, pair, :].rearrange("p a (o u) -> p a o u", u=2),
+                in_=flipped[:].rearrange("p a u o -> p a o u"),
+            )
+            nc.vector.quantize_mx(
+                out=w_codes[m][:, pair, :].rearrange("p a o -> p (a o)").bitcast(FP8X4),
+                scales=w_scales[m][:, pair, :].rearrange("p a o -> p (a o)"),
+                in_=grouped_w[m][:, pair, :].rearrange("p a f -> p (a f)"),
+            )
+
+        grouped = {}
+
+        def regroup(j):
+            grouped[j] = stage.tile([P, HALF_PIX, PACK], BF16, name="grouped", align_bytes=64)
             for cols, engine_copy in (
                 (slice(0, VECTOR_PIX), nc.vector.tensor_copy),
                 (slice(VECTOR_PIX, HALF_PIX), nc.scalar.copy),
             ):
                 engine_copy(
-                    out=grouped[:, cols, :].rearrange("p (c i) j -> p c j i", i=4),
-                    in_=raw[:, :, cols].rearrange("p j (c i) -> p c j i", i=4),
+                    out=grouped[j][:, cols, :].rearrange("p (c i) j -> p c j i", i=4),
+                    in_=x_raw[j][:, :, cols].rearrange("p j (c i) -> p c j i", i=4),
                 )
+
+        def quantise(j):
+            n, g, half = j // 4, (j // 2) % 2, j % 2
             first = half * HALF_PIX
             nc.vector.quantize_mx(
                 out=x_codes[n][:, g, WIDTH + first : WIDTH + first + HALF_PIX].bitcast(FP8X4),
                 scales=x_scales[n][:, g, first : first + HALF_PIX],
-                in_=grouped[:].rearrange("p w j -> p (w j)"),
+                in_=grouped[j][:].rearrange("p w j -> p (w j)"),
             )
+
+        def move_scales(j):
+            n, g = j // 4, (j // 2) % 2
             nc.vector.tensor_copy(
-                out=x_scales_pad[n][:, g, WIDTH + first : WIDTH + first + HALF_PIX].bitcast(I32),
-                in_=x_scales[n][:, g, first : first + HALF_PIX].bitcast(I32),
+                out=x_scales_pad[n][:, g, WIDTH : WIDTH + IMAGE_PIX].bitcast(I32),
+                in_=x_scales[n][:, g, :].bitcast(I32),
             )
 
-        def tap_passes(acc, n, m, half, taps):
-            last = len(taps) * PASSES - 1
-            count = 0
-            for tap in taps:
-                first_row = half * HALF_ROWS + ROW_OFFSET[tap]
-                first = (first_row + 1) * WIDTH
-                for g in range(PASSES):
-                    if first_row % 2 == 0:
-                        plane = x_scales[n][:, g, first - WIDTH : first - WIDTH + HALF_PIX]
-                    else:
-                        plane = x_scales_pad[n][:, g, first : first + HALF_PIX]
-                    nc.tensor.matmul_mx(
-                        out=acc[:].rearrange("o h w -> o (h w)"),
-                        lhsT=w_codes[m][:, g * TAPS + tap, :].bitcast(FP8X4),
-                        lhsT_scale=w_scales[m][:, g * TAPS + tap, :],
-                        rhs=x_codes[n][:, g, first : first + HALF_PIX].bitcast(FP8X4),
-                        rhs_scale=plane,
-                        start=(count == 0),
-                        stop=(count == last),
-                    )
-                    count += 1
+        acc = {}
+        result = {}
 
-        def convolve(n, m, half):
-            acc_mid = acc_pool.tile([P, HALF_ROWS, WIDTH], F32, name="acc_mid")
-            tap_passes(acc_mid, n, m, half, (CENTRE, UP, DOWN))
-            acc_left = acc_pool.tile([P, HALF_ROWS, WIDTH], F32, name="acc_left")
-            tap_passes(acc_left, n, m, half, (LEFT,))
-            acc_right = acc_pool.tile([P, HALF_ROWS, WIDTH], F32, name="acc_right")
-            tap_passes(acc_right, n, m, half, (RIGHT,))
-            result = stage.tile([P, HALF_ROWS, WIDTH], F32, name="result")
-            nc.scalar.copy(out=result[:], in_=acc_mid[:])
+        def matmuls(t):
+            n, m, g = t // 4, (t // 2) % 2, t % 2
+            for half in range(HALVES):
+                e = (t // 2) * HALVES + half
+                for taps in (MID_TAPS, LEFT_TAPS, RIGHT_TAPS):
+                    if g == 0:
+                        acc[e, taps] = psum.tile([P, HALF_ROWS, WIDTH], F32, name="acc", tag="bank")
+                    for tap in taps:
+                        first_row = half * HALF_ROWS + ROW_OFFSET[tap]
+                        first = (first_row + 1) * WIDTH
+                        if first_row % 2 == 0:
+                            plane = x_scales[n][:, g, first - WIDTH : first - WIDTH + HALF_PIX]
+                        else:
+                            plane = x_scales_pad[n][:, g, first : first + HALF_PIX]
+                        nc.tensor.matmul_mx(
+                            out=acc[e, taps][:].rearrange("o h w -> o (h w)"),
+                            lhsT=w_codes[m][:, g * TAPS + tap, :].bitcast(FP8X4),
+                            lhsT_scale=w_scales[m][:, g * TAPS + tap, :],
+                            rhs=x_codes[n][:, g, first : first + HALF_PIX].bitcast(FP8X4),
+                            rhs_scale=plane,
+                            start=(g == 0 and tap == taps[0]),
+                            stop=(g == PASSES - 1 and tap == taps[-1]),
+                        )
+                    if g == PASSES - 1 and taps == MID_TAPS:
+                        result[e] = stage.tile([P, HALF_ROWS, WIDTH], F32, name="result")
+                        nc.scalar.copy(out=result[e][:], in_=acc[e, taps][:])
+
+        def add_left(e):
             nc.vector.tensor_tensor(
-                out=result[:, :, 1:WIDTH],
-                in0=acc_left[:, :, 0 : WIDTH - 1],
-                in1=result[:, :, 1:WIDTH],
+                out=result[e][:, :, 1:WIDTH],
+                in0=acc[e, LEFT_TAPS][:, :, 0 : WIDTH - 1],
+                in1=result[e][:, :, 1:WIDTH],
                 op=ADD,
             )
+
+        def add_right_and_store(e):
+            n, m, half = e // 4, (e // 2) % 2, e % 2
             nc.vector.tensor_tensor(
-                out=result[:, :, 0 : WIDTH - 1],
-                in0=acc_right[:, :, 1:WIDTH],
-                in1=result[:, :, 0 : WIDTH - 1],
+                out=result[e][:, :, 0 : WIDTH - 1],
+                in0=acc[e, RIGHT_TAPS][:, :, 1:WIDTH],
+                in1=result[e][:, :, 0 : WIDTH - 1],
                 op=ADD,
             )
             nc.sync.dma_start(
                 out=out[n, m * P : (m + 1) * P, half * HALF_ROWS : (half + 1) * HALF_ROWS, :],
-                in_=result[:],
+                in_=result[e][:],
             )
 
-        pieces = [(half, g) for half in range(HALVES) for g in range(PASSES)]
-        rounds = [(m, half) for m in range(O_TILES) for half in range(HALVES)]
-        prepare_weights(0)
-        for half, g in pieces:
-            prepare_piece(0, half, g)
-        for n in range(IMAGES):
-            for (m, half), (next_half, next_g) in zip(rounds, pieces):
-                convolve(n, m, half)
-                if n == 0 and half == 0 and m + 1 < O_TILES:
-                    prepare_weights(m + 1)
-                if n + 1 < IMAGES:
-                    prepare_piece(n + 1, next_half, next_g)
+        for m in range(O_TILES):
+            for g in range(PASSES):
+                sort_weights(m, g)
+        for m in range(O_TILES):
+            for first in range(0, OPERANDS, 2):
+                flip_weights(m, first)
+        for t in range(-4, STEPS + 2):
+            e = t - 2
+            if 0 <= t + 3 < PIECES:
+                quantise(t + 3)
+            if 0 <= e < ROUNDS:
+                add_left(e)
+            if 0 <= t + 4 < PIECES:
+                regroup(t + 4)
+            if 0 <= e < ROUNDS:
+                add_right_and_store(e)
+            if 0 <= t + 3 < PIECES and (t + 3) % HALVES == HALVES - 1:
+                move_scales(t + 3)
+            if 0 <= t < STEPS:
+                matmuls(t)

@@ -21,19 +21,13 @@ O_TILES = C_OUT // P
 HALVES = 2
 HALF_ROWS = HEIGHT // HALVES
 HALF_PIX = HALF_ROWS * WIDTH
-IMAGE_PIX = HEIGHT * WIDTH
 PAD_PIX = (HEIGHT + 2) * WIDTH
 OPERANDS = PASSES * TAPS
-PSUM_BANKS = 8
 
 CENTRE, UP, LEFT, RIGHT, DOWN = 0, 1, 2, 3, 4
 ROW_OFFSET = {CENTRE: 0, UP: -1, LEFT: 0, RIGHT: 0, DOWN: 1}
-MID_TAPS, LEFT_TAPS, RIGHT_TAPS = (CENTRE, UP, DOWN), (LEFT,), (RIGHT,)
 
-STEPS = IMAGES * O_TILES * PASSES
-PIECES = IMAGES * PASSES * HALVES
-ROUNDS = IMAGES * O_TILES * HALVES
-
+VECTOR_TAPS = 3
 VECTOR_PIX = 192
 
 FLOPS = 2 * IMAGES * HEIGHT * WIDTH * C_IN * C_OUT * TAPS
@@ -44,11 +38,13 @@ def tile_spatialconv_pa_t_kernel(tc, x, weight, out):
     with ExitStack() as ctx:
         keep = ctx.enter_context(tc.tile_pool(name="keep", bufs=1))
         stage = ctx.enter_context(tc.tile_pool(name="stage", bufs=4))
-        psum = ctx.enter_context(tc.psum_pool(name="psum", bufs=PSUM_BANKS))
-        ctx.enter_context(tc.manual_schedule())
+        acc_pool = ctx.enter_context(tc.psum_pool(name="acc", bufs=2))
+        flip_pool = ctx.enter_context(tc.psum_pool(name="flip", bufs=2))
 
         w_raw = {}
-        for m in range(O_TILES):
+        x_raw = {}
+
+        def load_weights(m):
             for g in range(PASSES):
                 w_raw[m, g] = keep.tile([P, K_PASS * TAPS], BF16, name="w_raw_%d_%d" % (m, g))
                 nc.sync.dma_start(
@@ -57,16 +53,28 @@ def tile_spatialconv_pa_t_kernel(tc, x, weight, out):
                         "o c k -> o (c k)"
                     ),
                 )
-        x_raw = {}
-        for j in range(PIECES):
-            n, g, half = j // 4, (j // 2) % 2, j % 2
-            x_raw[j] = keep.tile([P, PACK, HALF_PIX], BF16, name="x_raw_%d" % j)
-            nc.sync.dma_start(
-                out=x_raw[j][:],
-                in_=x[
-                    n, g * K_PASS : (g + 1) * K_PASS, half * HALF_ROWS : (half + 1) * HALF_ROWS, :
-                ].rearrange("(p j) h w -> p j (h w)", j=PACK),
-            )
+
+        def load_image(n):
+            for half in range(HALVES):
+                for g in range(PASSES):
+                    x_raw[n, half, g] = keep.tile(
+                        [P, PACK, HALF_PIX], BF16, name="x_raw_%d_%d_%d" % (n, half, g)
+                    )
+                    nc.sync.dma_start(
+                        out=x_raw[n, half, g][:],
+                        in_=x[
+                            n,
+                            g * K_PASS : (g + 1) * K_PASS,
+                            half * HALF_ROWS : (half + 1) * HALF_ROWS,
+                            :,
+                        ].rearrange("(p j) h w -> p j (h w)", j=PACK),
+                    )
+
+        load_weights(0)
+        load_image(0)
+        load_weights(1)
+        for n in range(1, IMAGES):
+            load_image(n)
 
         ident = keep.tile([P, P], F32, name="ident")
         make_identity(nc, ident[:])
@@ -76,7 +84,9 @@ def tile_spatialconv_pa_t_kernel(tc, x, weight, out):
         x_scales_pad = {}
         for n in range(IMAGES):
             x_codes[n] = keep.tile([P, PASSES, PAD_PIX], U32, name="x_codes_%d" % n, align_bytes=64)
-            x_scales[n] = keep.tile([P, PASSES, IMAGE_PIX], U8, name="x_scales_%d" % n, align_bytes=64)
+            x_scales[n] = keep.tile(
+                [P, PASSES, HEIGHT * WIDTH], U8, name="x_scales_%d" % n, align_bytes=64
+            )
             x_scales_pad[n] = keep.tile(
                 [P, PASSES, PAD_PIX], U8, name="x_scales_pad_%d" % n, align_bytes=64
             )
@@ -85,143 +95,119 @@ def tile_spatialconv_pa_t_kernel(tc, x, weight, out):
             nc.vector.memset(x_codes[n][:, :, 0:WIDTH].bitcast(I32), 0)
             nc.vector.memset(x_codes[n][:, :, PAD_PIX - WIDTH : PAD_PIX].bitcast(I32), 0)
 
-        sorted_w = {}
-        grouped_w = {}
         w_codes = {}
         w_scales = {}
-        for m in range(O_TILES):
-            sorted_w[m] = keep.tile([P, OPERANDS, 2, 2 * P], BF16, name="sorted_w_%d" % m)
-            grouped_w[m] = keep.tile(
-                [P, OPERANDS, PACK * P], BF16, name="grouped_w_%d" % m, align_bytes=64
-            )
+
+        def prepare_weights(m):
+            sorted_w = keep.tile([P, OPERANDS, K_PASS], BF16, name="sorted_w_%d" % m)
+            for g in range(PASSES):
+                by_channel = w_raw[m, g][:].rearrange("o (c k) -> o c k", k=TAPS)
+                by_tap = sorted_w[:, g * TAPS : (g + 1) * TAPS, :].rearrange("o k c -> o c k")
+                nc.vector.tensor_copy(out=by_tap[:, :, 0:VECTOR_TAPS], in_=by_channel[:, :, 0:VECTOR_TAPS])
+                nc.scalar.copy(out=by_tap[:, :, VECTOR_TAPS:TAPS], in_=by_channel[:, :, VECTOR_TAPS:TAPS])
+            sorted_words = sorted_w[:].bitcast(F32).rearrange("o a (p u) -> o a u p", u=2)
+            grouped_w = keep.tile([P, OPERANDS, PACK * P], BF16, name="grouped_w_%d" % m, align_bytes=64)
+            grouped_words = grouped_w[:].bitcast(F32)
             w_codes[m] = keep.tile([P, OPERANDS, P], U32, name="w_codes_%d" % m, align_bytes=64)
             w_scales[m] = keep.tile([P, OPERANDS, P], U8, name="w_scales_%d" % m, align_bytes=64)
+            for first in range(0, OPERANDS, 2):
+                pair = slice(first, first + 2)
+                flipped = flip_pool.tile([P, 2, 2, P], F32, name="flipped")
+                for a in range(2):
+                    for u in range(2):
+                        nc.tensor.transpose(
+                            out=flipped[:, a, u, :], in_=sorted_words[:, first + a, u, :], identity=ident[:]
+                        )
+                engine_copy = nc.scalar.copy if first % 4 == 0 else nc.vector.tensor_copy
+                engine_copy(
+                    out=grouped_words[:, pair, :].rearrange("p a (o u) -> p a o u", u=2),
+                    in_=flipped[:].rearrange("p a u o -> p a o u"),
+                )
+                nc.vector.quantize_mx(
+                    out=w_codes[m][:, pair, :].rearrange("p a o -> p (a o)").bitcast(FP8X4),
+                    scales=w_scales[m][:, pair, :].rearrange("p a o -> p (a o)"),
+                    in_=grouped_w[:, pair, :].rearrange("p a f -> p (a f)"),
+                )
 
-        def sort_weights(m, g):
-            nc.vector.tensor_copy(
-                out=sorted_w[m][:, g * TAPS : (g + 1) * TAPS, :, :].rearrange(
-                    "o k u (p e) -> o k u p e", e=2
-                ),
-                in_=w_raw[m, g][:].rearrange("o (p u e k) -> o k u p e", u=2, e=2, k=TAPS),
-            )
-
-        def flip_weights(m, first):
-            pair = slice(first, first + 2)
-            flipped = psum.tile([P, 2, 2, P], F32, name="flipped", tag="bank")
-            for a in range(2):
-                for u in range(2):
-                    nc.tensor.transpose(
-                        out=flipped[:, a, u, :],
-                        in_=sorted_w[m][:].bitcast(F32)[:, first + a, u, :],
-                        identity=ident[:],
-                    )
-            nc.scalar.copy(
-                out=grouped_w[m][:].bitcast(F32)[:, pair, :].rearrange("p a (o u) -> p a o u", u=2),
-                in_=flipped[:].rearrange("p a u o -> p a o u"),
-            )
-            nc.vector.quantize_mx(
-                out=w_codes[m][:, pair, :].rearrange("p a o -> p (a o)").bitcast(FP8X4),
-                scales=w_scales[m][:, pair, :].rearrange("p a o -> p (a o)"),
-                in_=grouped_w[m][:, pair, :].rearrange("p a f -> p (a f)"),
-            )
-
-        grouped = {}
-
-        def regroup(j):
-            grouped[j] = stage.tile([P, HALF_PIX, PACK], BF16, name="grouped", align_bytes=64)
+        def prepare_piece(n, half, g):
+            raw = x_raw[n, half, g]
+            grouped = stage.tile([P, HALF_PIX, PACK], BF16, name="grouped", align_bytes=64)
             for cols, engine_copy in (
                 (slice(0, VECTOR_PIX), nc.vector.tensor_copy),
                 (slice(VECTOR_PIX, HALF_PIX), nc.scalar.copy),
             ):
                 engine_copy(
-                    out=grouped[j][:, cols, :].rearrange("p (c i) j -> p c j i", i=4),
-                    in_=x_raw[j][:, :, cols].rearrange("p j (c i) -> p c j i", i=4),
+                    out=grouped[:, cols, :].rearrange("p (c i) j -> p c j i", i=4),
+                    in_=raw[:, :, cols].rearrange("p j (c i) -> p c j i", i=4),
                 )
-
-        def quantise(j):
-            n, g, half = j // 4, (j // 2) % 2, j % 2
             first = half * HALF_PIX
             nc.vector.quantize_mx(
                 out=x_codes[n][:, g, WIDTH + first : WIDTH + first + HALF_PIX].bitcast(FP8X4),
                 scales=x_scales[n][:, g, first : first + HALF_PIX],
-                in_=grouped[j][:].rearrange("p w j -> p (w j)"),
+                in_=grouped[:].rearrange("p w j -> p (w j)"),
             )
-
-        def move_scales(j):
-            n, g = j // 4, (j // 2) % 2
             nc.vector.tensor_copy(
-                out=x_scales_pad[n][:, g, WIDTH : WIDTH + IMAGE_PIX].bitcast(I32),
-                in_=x_scales[n][:, g, :].bitcast(I32),
+                out=x_scales_pad[n][:, g, WIDTH + first : WIDTH + first + HALF_PIX].bitcast(I32),
+                in_=x_scales[n][:, g, first : first + HALF_PIX].bitcast(I32),
             )
 
-        acc = {}
-        result = {}
+        def tap_passes(acc, n, m, half, taps):
+            last = len(taps) * PASSES - 1
+            count = 0
+            for tap in taps:
+                first_row = half * HALF_ROWS + ROW_OFFSET[tap]
+                first = (first_row + 1) * WIDTH
+                for g in range(PASSES):
+                    if first_row % 2 == 0:
+                        plane = x_scales[n][:, g, first - WIDTH : first - WIDTH + HALF_PIX]
+                    else:
+                        plane = x_scales_pad[n][:, g, first : first + HALF_PIX]
+                    nc.tensor.matmul_mx(
+                        out=acc[:].rearrange("o h w -> o (h w)"),
+                        lhsT=w_codes[m][:, g * TAPS + tap, :].bitcast(FP8X4),
+                        lhsT_scale=w_scales[m][:, g * TAPS + tap, :],
+                        rhs=x_codes[n][:, g, first : first + HALF_PIX].bitcast(FP8X4),
+                        rhs_scale=plane,
+                        start=(count == 0),
+                        stop=(count == last),
+                    )
+                    count += 1
 
-        def matmuls(t):
-            n, m, g = t // 4, (t // 2) % 2, t % 2
-            for half in range(HALVES):
-                e = (t // 2) * HALVES + half
-                for taps in (MID_TAPS, LEFT_TAPS, RIGHT_TAPS):
-                    if g == 0:
-                        acc[e, taps] = psum.tile([P, HALF_ROWS, WIDTH], F32, name="acc", tag="bank")
-                    for tap in taps:
-                        first_row = half * HALF_ROWS + ROW_OFFSET[tap]
-                        first = (first_row + 1) * WIDTH
-                        if first_row % 2 == 0:
-                            plane = x_scales[n][:, g, first - WIDTH : first - WIDTH + HALF_PIX]
-                        else:
-                            plane = x_scales_pad[n][:, g, first : first + HALF_PIX]
-                        nc.tensor.matmul_mx(
-                            out=acc[e, taps][:].rearrange("o h w -> o (h w)"),
-                            lhsT=w_codes[m][:, g * TAPS + tap, :].bitcast(FP8X4),
-                            lhsT_scale=w_scales[m][:, g * TAPS + tap, :],
-                            rhs=x_codes[n][:, g, first : first + HALF_PIX].bitcast(FP8X4),
-                            rhs_scale=plane,
-                            start=(g == 0 and tap == taps[0]),
-                            stop=(g == PASSES - 1 and tap == taps[-1]),
-                        )
-                    if g == PASSES - 1 and taps == MID_TAPS:
-                        result[e] = stage.tile([P, HALF_ROWS, WIDTH], F32, name="result")
-                        nc.scalar.copy(out=result[e][:], in_=acc[e, taps][:])
-
-        def add_left(e):
+        def convolve(n, m, half):
+            acc_mid = acc_pool.tile([P, HALF_ROWS, WIDTH], F32, name="acc_mid")
+            tap_passes(acc_mid, n, m, half, (CENTRE, UP, DOWN))
+            acc_left = acc_pool.tile([P, HALF_ROWS, WIDTH], F32, name="acc_left")
+            tap_passes(acc_left, n, m, half, (LEFT,))
+            acc_right = acc_pool.tile([P, HALF_ROWS, WIDTH], F32, name="acc_right")
+            tap_passes(acc_right, n, m, half, (RIGHT,))
+            result = stage.tile([P, HALF_ROWS, WIDTH], F32, name="result")
+            nc.scalar.copy(out=result[:], in_=acc_mid[:])
             nc.vector.tensor_tensor(
-                out=result[e][:, :, 1:WIDTH],
-                in0=acc[e, LEFT_TAPS][:, :, 0 : WIDTH - 1],
-                in1=result[e][:, :, 1:WIDTH],
+                out=result[:, :, 1:WIDTH],
+                in0=acc_left[:, :, 0 : WIDTH - 1],
+                in1=result[:, :, 1:WIDTH],
                 op=ADD,
             )
-
-        def add_right_and_store(e):
-            n, m, half = e // 4, (e // 2) % 2, e % 2
             nc.vector.tensor_tensor(
-                out=result[e][:, :, 0 : WIDTH - 1],
-                in0=acc[e, RIGHT_TAPS][:, :, 1:WIDTH],
-                in1=result[e][:, :, 0 : WIDTH - 1],
+                out=result[:, :, 0 : WIDTH - 1],
+                in0=acc_right[:, :, 1:WIDTH],
+                in1=result[:, :, 0 : WIDTH - 1],
                 op=ADD,
             )
             nc.sync.dma_start(
                 out=out[n, m * P : (m + 1) * P, half * HALF_ROWS : (half + 1) * HALF_ROWS, :],
-                in_=result[e][:],
+                in_=result[:],
             )
 
-        for m in range(O_TILES):
-            for g in range(PASSES):
-                sort_weights(m, g)
-        for m in range(O_TILES):
-            for first in range(0, OPERANDS, 2):
-                flip_weights(m, first)
-        for t in range(-4, STEPS + 2):
-            e = t - 2
-            if 0 <= t + 3 < PIECES:
-                quantise(t + 3)
-            if 0 <= e < ROUNDS:
-                add_left(e)
-            if 0 <= t + 4 < PIECES:
-                regroup(t + 4)
-            if 0 <= e < ROUNDS:
-                add_right_and_store(e)
-            if 0 <= t + 3 < PIECES and (t + 3) % HALVES == HALVES - 1:
-                move_scales(t + 3)
-            if 0 <= t < STEPS:
-                matmuls(t)
+        pieces = [(half, g) for half in range(HALVES) for g in range(PASSES)]
+        rounds = [(m, half) for m in range(O_TILES) for half in range(HALVES)]
+        prepare_weights(0)
+        for half, g in pieces:
+            prepare_piece(0, half, g)
+        for n in range(IMAGES):
+            for (m, half), (next_half, next_g) in zip(rounds, pieces):
+                convolve(n, m, half)
+                if n == 0 and half == 0 and m + 1 < O_TILES:
+                    prepare_weights(m + 1)
+                if n + 1 < IMAGES:
+                    prepare_piece(n + 1, next_half, next_g)

@@ -21,6 +21,7 @@ O_TILES = C_OUT // P
 HALVES = 2
 HALF_ROWS = HEIGHT // HALVES
 HALF_PIX = HALF_ROWS * WIDTH
+IMAGE_PIX = HEIGHT * WIDTH
 PAD_PIX = (HEIGHT + 2) * WIDTH
 OPERANDS = PASSES * TAPS
 
@@ -55,20 +56,14 @@ def tile_spatialconv_pa_t_kernel(tc, x, weight, out):
                 )
 
         def load_image(n):
-            for half in range(HALVES):
-                for g in range(PASSES):
-                    x_raw[n, half, g] = keep.tile(
-                        [P, PACK, HALF_PIX], BF16, name="x_raw_%d_%d_%d" % (n, half, g)
-                    )
-                    nc.sync.dma_start(
-                        out=x_raw[n, half, g][:],
-                        in_=x[
-                            n,
-                            g * K_PASS : (g + 1) * K_PASS,
-                            half * HALF_ROWS : (half + 1) * HALF_ROWS,
-                            :,
-                        ].rearrange("(p j) h w -> p j (h w)", j=PACK),
-                    )
+            for g in range(PASSES):
+                x_raw[n, g] = keep.tile([P, PACK, IMAGE_PIX], BF16, name="x_raw_%d_%d" % (n, g))
+                nc.sync.dma_start(
+                    out=x_raw[n, g][:].rearrange("p (u e) w -> p u (e w)", e=2),
+                    in_=x[n, g * K_PASS : (g + 1) * K_PASS, :, :].rearrange(
+                        "(u p e) h w -> p u (e h w)", u=2, e=2
+                    ),
+                )
 
         load_weights(0)
         load_image(0)
@@ -84,16 +79,14 @@ def tile_spatialconv_pa_t_kernel(tc, x, weight, out):
         x_scales_pad = {}
         for n in range(IMAGES):
             x_codes[n] = keep.tile([P, PASSES, PAD_PIX], U32, name="x_codes_%d" % n, align_bytes=64)
-            x_scales[n] = keep.tile(
-                [P, PASSES, HEIGHT * WIDTH], U8, name="x_scales_%d" % n, align_bytes=64
-            )
+            x_scales[n] = keep.tile([P, PASSES, IMAGE_PIX], U8, name="x_scales_%d" % n, align_bytes=64)
             x_scales_pad[n] = keep.tile(
                 [P, PASSES, PAD_PIX], U8, name="x_scales_pad_%d" % n, align_bytes=64
             )
             nc.vector.memset(x_scales[n][:].bitcast(I32), 0)
-            nc.vector.memset(x_scales_pad[n][:].bitcast(I32), 0)
-            nc.vector.memset(x_codes[n][:, :, 0:WIDTH].bitcast(I32), 0)
-            nc.vector.memset(x_codes[n][:, :, PAD_PIX - WIDTH : PAD_PIX].bitcast(I32), 0)
+            for pad_row in (slice(0, WIDTH), slice(PAD_PIX - WIDTH, PAD_PIX)):
+                nc.vector.memset(x_codes[n][:, :, pad_row].bitcast(I32), 0)
+                nc.vector.memset(x_scales_pad[n][:, :, pad_row].bitcast(I32), 0)
 
         w_codes = {}
         w_scales = {}
@@ -105,7 +98,7 @@ def tile_spatialconv_pa_t_kernel(tc, x, weight, out):
                 by_tap = sorted_w[:, g * TAPS : (g + 1) * TAPS, :].rearrange("o k c -> o c k")
                 nc.vector.tensor_copy(out=by_tap[:, :, 0:VECTOR_TAPS], in_=by_channel[:, :, 0:VECTOR_TAPS])
                 nc.scalar.copy(out=by_tap[:, :, VECTOR_TAPS:TAPS], in_=by_channel[:, :, VECTOR_TAPS:TAPS])
-            sorted_words = sorted_w[:].bitcast(F32).rearrange("o a (p u) -> o a u p", u=2)
+            sorted_words = sorted_w[:].bitcast(F32).rearrange("o a (u p) -> o a u p", u=2)
             grouped_w = keep.tile([P, OPERANDS, PACK * P], BF16, name="grouped_w_%d" % m, align_bytes=64)
             grouped_words = grouped_w[:].bitcast(F32)
             w_codes[m] = keep.tile([P, OPERANDS, P], U32, name="w_codes_%d" % m, align_bytes=64)
@@ -118,8 +111,7 @@ def tile_spatialconv_pa_t_kernel(tc, x, weight, out):
                         nc.tensor.transpose(
                             out=flipped[:, a, u, :], in_=sorted_words[:, first + a, u, :], identity=ident[:]
                         )
-                engine_copy = nc.scalar.copy if first % 4 == 0 else nc.vector.tensor_copy
-                engine_copy(
+                nc.scalar.copy(
                     out=grouped_words[:, pair, :].rearrange("p a (o u) -> p a o u", u=2),
                     in_=flipped[:].rearrange("p a u o -> p a o u"),
                 )
@@ -130,26 +122,28 @@ def tile_spatialconv_pa_t_kernel(tc, x, weight, out):
                 )
 
         def prepare_piece(n, half, g):
-            raw = x_raw[n, half, g]
+            first = half * HALF_PIX
             grouped = stage.tile([P, HALF_PIX, PACK], BF16, name="grouped", align_bytes=64)
-            for cols, engine_copy in (
-                (slice(0, VECTOR_PIX), nc.vector.tensor_copy),
-                (slice(VECTOR_PIX, HALF_PIX), nc.scalar.copy),
+            for start, stop, engine_copy in (
+                (0, VECTOR_PIX, nc.vector.tensor_copy),
+                (VECTOR_PIX, HALF_PIX, nc.scalar.copy),
             ):
                 engine_copy(
-                    out=grouped[:, cols, :].rearrange("p (c i) j -> p c j i", i=4),
-                    in_=raw[:, :, cols].rearrange("p j (c i) -> p c j i", i=4),
+                    out=grouped[:, start:stop, :].rearrange("p (c i) t -> p c t i", i=4),
+                    in_=x_raw[n, g][:, :, first + start : first + stop].rearrange(
+                        "p t (c i) -> p c t i", i=4
+                    ),
                 )
-            first = half * HALF_PIX
             nc.vector.quantize_mx(
                 out=x_codes[n][:, g, WIDTH + first : WIDTH + first + HALF_PIX].bitcast(FP8X4),
                 scales=x_scales[n][:, g, first : first + HALF_PIX],
-                in_=grouped[:].rearrange("p w j -> p (w j)"),
+                in_=grouped[:].rearrange("p w t -> p (w t)"),
             )
-            nc.vector.tensor_copy(
-                out=x_scales_pad[n][:, g, WIDTH + first : WIDTH + first + HALF_PIX].bitcast(I32),
-                in_=x_scales[n][:, g, first : first + HALF_PIX].bitcast(I32),
-            )
+            if g == PASSES - 1:
+                nc.vector.tensor_copy(
+                    out=x_scales_pad[n][:, :, WIDTH + first : WIDTH + first + HALF_PIX].bitcast(I32),
+                    in_=x_scales[n][:, :, first : first + HALF_PIX].bitcast(I32),
+                )
 
         def tap_passes(acc, n, m, half, taps):
             last = len(taps) * PASSES - 1

@@ -29,7 +29,7 @@ CENTRE, UP, LEFT, RIGHT, DOWN = 0, 1, 2, 3, 4
 ROW_OFFSET = {CENTRE: 0, UP: -1, LEFT: 0, RIGHT: 0, DOWN: 1}
 
 VECTOR_TAPS = 3
-VECTOR_PIX = 192
+VECTOR_PIX = 256
 
 FLOPS = 2 * IMAGES * HEIGHT * WIDTH * C_IN * C_OUT * TAPS
 

from contextlib import ExitStack

import concourse.mybir as mybir
from concourse.masks import make_identity

BF16 = mybir.dt.bfloat16
F32 = mybir.dt.float32
I32 = mybir.dt.int32
U32 = mybir.dt.uint32
U8 = mybir.dt.uint8
FP8X4 = mybir.dt.float8_e4m3fn_x4
ADD = mybir.AluOpType.add

IMAGES, C_IN, HEIGHT, WIDTH = 4, 1024, 32, 32
C_OUT, TAPS = 256, 5
P = 128
PACK = 4
K_PASS = P * PACK
PASSES = C_IN // K_PASS
O_TILES = C_OUT // P
HALVES = 2
HALF_ROWS = HEIGHT // HALVES
HALF_PIX = HALF_ROWS * WIDTH
IMAGE_PIX = HEIGHT * WIDTH
PAD_PIX = (HEIGHT + 2) * WIDTH
OPERANDS = PASSES * TAPS

CENTRE, UP, LEFT, RIGHT, DOWN = 0, 1, 2, 3, 4
ROW_OFFSET = {CENTRE: 0, UP: -1, LEFT: 0, RIGHT: 0, DOWN: 1}

VECTOR_TAPS = 3
VECTOR_PIX = 256

FLOPS = 2 * IMAGES * HEIGHT * WIDTH * C_IN * C_OUT * TAPS


def tile_spatialconv_pa_t_kernel(tc, x, weight, out):
    nc = tc.nc
    with ExitStack() as ctx:
        keep = ctx.enter_context(tc.tile_pool(name="keep", bufs=1))
        stage = ctx.enter_context(tc.tile_pool(name="stage", bufs=4))
        acc_pool = ctx.enter_context(tc.psum_pool(name="acc", bufs=2))
        flip_pool = ctx.enter_context(tc.psum_pool(name="flip", bufs=2))

        w_raw = {}
        x_raw = {}

        def load_weights(m):
            for g in range(PASSES):
                w_raw[m, g] = keep.tile([P, K_PASS * TAPS], BF16, name="w_raw_%d_%d" % (m, g))
                nc.sync.dma_start(
                    out=w_raw[m, g][:],
                    in_=weight[m * P : (m + 1) * P, g * K_PASS : (g + 1) * K_PASS, :].rearrange(
                        "o c k -> o (c k)"
                    ),
                )

        def load_image(n):
            for g in range(PASSES):
                x_raw[n, g] = keep.tile([P, PACK, IMAGE_PIX], BF16, name="x_raw_%d_%d" % (n, g))
                nc.sync.dma_start(
                    out=x_raw[n, g][:].rearrange("p (u e) w -> p u (e w)", e=2),
                    in_=x[n, g * K_PASS : (g + 1) * K_PASS, :, :].rearrange(
                        "(u p e) h w -> p u (e h w)", u=2, e=2
                    ),
                )

        load_weights(0)
        load_image(0)
        load_weights(1)
        for n in range(1, IMAGES):
            load_image(n)

        ident = keep.tile([P, P], F32, name="ident")
        make_identity(nc, ident[:])

        x_codes = {}
        x_scales = {}
        x_scales_pad = {}
        for n in range(IMAGES):
            x_codes[n] = keep.tile([P, PASSES, PAD_PIX], U32, name="x_codes_%d" % n, align_bytes=64)
            x_scales[n] = keep.tile([P, PASSES, IMAGE_PIX], U8, name="x_scales_%d" % n, align_bytes=64)
            x_scales_pad[n] = keep.tile(
                [P, PASSES, PAD_PIX], U8, name="x_scales_pad_%d" % n, align_bytes=64
            )
            nc.vector.memset(x_scales[n][:].bitcast(I32), 0)
            for pad_row in (slice(0, WIDTH), slice(PAD_PIX - WIDTH, PAD_PIX)):
                nc.vector.memset(x_codes[n][:, :, pad_row].bitcast(I32), 0)
                nc.vector.memset(x_scales_pad[n][:, :, pad_row].bitcast(I32), 0)

        w_codes = {}
        w_scales = {}

        def prepare_weights(m):
            sorted_w = keep.tile([P, OPERANDS, K_PASS], BF16, name="sorted_w_%d" % m)
            for g in range(PASSES):
                by_channel = w_raw[m, g][:].rearrange("o (c k) -> o c k", k=TAPS)
                by_tap = sorted_w[:, g * TAPS : (g + 1) * TAPS, :].rearrange("o k c -> o c k")
                nc.vector.tensor_copy(out=by_tap[:, :, 0:VECTOR_TAPS], in_=by_channel[:, :, 0:VECTOR_TAPS])
                nc.scalar.copy(out=by_tap[:, :, VECTOR_TAPS:TAPS], in_=by_channel[:, :, VECTOR_TAPS:TAPS])
            sorted_words = sorted_w[:].bitcast(F32).rearrange("o a (u p) -> o a u p", u=2)
            grouped_w = keep.tile([P, OPERANDS, PACK * P], BF16, name="grouped_w_%d" % m, align_bytes=64)
            grouped_words = grouped_w[:].bitcast(F32)
            w_codes[m] = keep.tile([P, OPERANDS, P], U32, name="w_codes_%d" % m, align_bytes=64)
            w_scales[m] = keep.tile([P, OPERANDS, P], U8, name="w_scales_%d" % m, align_bytes=64)
            for first in range(0, OPERANDS, 2):
                pair = slice(first, first + 2)
                flipped = flip_pool.tile([P, 2, 2, P], F32, name="flipped")
                for a in range(2):
                    for u in range(2):
                        nc.tensor.transpose(
                            out=flipped[:, a, u, :], in_=sorted_words[:, first + a, u, :], identity=ident[:]
                        )
                nc.scalar.copy(
                    out=grouped_words[:, pair, :].rearrange("p a (o u) -> p a o u", u=2),
                    in_=flipped[:].rearrange("p a u o -> p a o u"),
                )
                nc.vector.quantize_mx(
                    out=w_codes[m][:, pair, :].rearrange("p a o -> p (a o)").bitcast(FP8X4),
                    scales=w_scales[m][:, pair, :].rearrange("p a o -> p (a o)"),
                    in_=grouped_w[:, pair, :].rearrange("p a f -> p (a f)"),
                )

        def prepare_piece(n, half, g):
            first = half * HALF_PIX
            grouped = stage.tile([P, HALF_PIX, PACK], BF16, name="grouped", align_bytes=64)
            for start, stop, engine_copy in (
                (0, VECTOR_PIX, nc.vector.tensor_copy),
                (VECTOR_PIX, HALF_PIX, nc.scalar.copy),
            ):
                engine_copy(
                    out=grouped[:, start:stop, :].rearrange("p (c i) t -> p c t i", i=4),
                    in_=x_raw[n, g][:, :, first + start : first + stop].rearrange(
                        "p t (c i) -> p c t i", i=4
                    ),
                )
            nc.vector.quantize_mx(
                out=x_codes[n][:, g, WIDTH + first : WIDTH + first + HALF_PIX].bitcast(FP8X4),
                scales=x_scales[n][:, g, first : first + HALF_PIX],
                in_=grouped[:].rearrange("p w t -> p (w t)"),
            )
            if g == PASSES - 1:
                nc.vector.tensor_copy(
                    out=x_scales_pad[n][:, :, WIDTH + first : WIDTH + first + HALF_PIX].bitcast(I32),
                    in_=x_scales[n][:, :, first : first + HALF_PIX].bitcast(I32),
                )

        def tap_passes(acc, n, m, half, taps):
            last = len(taps) * PASSES - 1
            count = 0
            for tap in taps:
                first_row = half * HALF_ROWS + ROW_OFFSET[tap]
                first = (first_row + 1) * WIDTH
                for g in range(PASSES):
                    if first_row % 2 == 0:
                        plane = x_scales[n][:, g, first - WIDTH : first - WIDTH + HALF_PIX]
                    else:
                        plane = x_scales_pad[n][:, g, first : first + HALF_PIX]
                    nc.tensor.matmul_mx(
                        out=acc[:].rearrange("o h w -> o (h w)"),
                        lhsT=w_codes[m][:, g * TAPS + tap, :].bitcast(FP8X4),
                        lhsT_scale=w_scales[m][:, g * TAPS + tap, :],
                        rhs=x_codes[n][:, g, first : first + HALF_PIX].bitcast(FP8X4),
                        rhs_scale=plane,
                        start=(count == 0),
                        stop=(count == last),
                    )
                    count += 1

        def convolve(n, m, half):
            acc_mid = acc_pool.tile([P, HALF_ROWS, WIDTH], F32, name="acc_mid")
            tap_passes(acc_mid, n, m, half, (CENTRE, UP, DOWN))
            acc_left = acc_pool.tile([P, HALF_ROWS, WIDTH], F32, name="acc_left")
            tap_passes(acc_left, n, m, half, (LEFT,))
            acc_right = acc_pool.tile([P, HALF_ROWS, WIDTH], F32, name="acc_right")
            tap_passes(acc_right, n, m, half, (RIGHT,))
            result = stage.tile([P, HALF_ROWS, WIDTH], F32, name="result")
            nc.scalar.copy(out=result[:], in_=acc_mid[:])
            nc.vector.tensor_tensor(
                out=result[:, :, 1:WIDTH],
                in0=acc_left[:, :, 0 : WIDTH - 1],
                in1=result[:, :, 1:WIDTH],
                op=ADD,
            )
            nc.vector.tensor_tensor(
                out=result[:, :, 0 : WIDTH - 1],
                in0=acc_right[:, :, 1:WIDTH],
                in1=result[:, :, 0 : WIDTH - 1],
                op=ADD,
            )
            nc.sync.dma_start(
                out=out[n, m * P : (m + 1) * P, half * HALF_ROWS : (half + 1) * HALF_ROWS, :],
                in_=result[:],
            )

        pieces = [(half, g) for half in range(HALVES) for g in range(PASSES)]
        rounds = [(m, half) for m in range(O_TILES) for half in range(HALVES)]
        prepare_weights(0)
        for half, g in pieces:
            prepare_piece(0, half, g)
        for n in range(IMAGES):
            for (m, half), (next_half, next_g) in zip(rounds, pieces):
                convolve(n, m, half)
                if n == 0 and half == 0 and m + 1 < O_TILES:
                    prepare_weights(m + 1)
                if n + 1 < IMAGES:
                    prepare_piece(n + 1, next_half, next_g)
